import numpy as np
import ml_dtypes


def mxq(x, axis, fmt="e4m3"):
    dtype, down = {"e4m3": (ml_dtypes.float8_e4m3fn, 7), "e5m2": (ml_dtypes.float8_e5m2, 14)}[fmt]
    v = np.moveaxis(np.asarray(x, np.float32).astype(ml_dtypes.bfloat16).astype(np.float64), axis, -1)
    blocks = v.reshape(v.shape[:-1] + (-1, 32))
    amax = np.abs(blocks).max(-1, keepdims=True)
    byte = np.maximum(np.where(amax > 0, np.frexp(amax)[1] - 1 + 127, 0) - down, 1)
    scale = np.exp2(byte - 127.0)
    codes = (blocks / scale).astype(np.float32).astype(dtype).astype(np.float64)
    return np.moveaxis((codes * scale).reshape(v.shape), -1, axis)


WIDE = False


def mx_kscale(k):
    if not WIDE:
        return np.ones(k)
    levels = np.array([10, -10, 5, -5, 0])
    if k % 512:
        return np.exp2(np.random.permutation(np.resize(levels, k // 32))).repeat(32)
    a = np.empty((k // 512, 16))
    for p in range(k // 512):
        a[p, :8] = np.random.permutation(np.resize(levels, 8))
        for g in range(8):
            far = levels[np.abs(levels - a[p, g]) >= 10]
            a[p, g + 8] = far[np.random.randint(len(far))]
    return np.exp2(a.ravel()).repeat(32)


BF16 = ml_dtypes.bfloat16


def bf(x):
    return np.asarray(x, np.float32).astype(BF16)


def f64(x):
    return np.asarray(x).astype(np.float64)


B_, S, D_IN, D_OUT, N, RANK, ALPHA = 4, 2048, 512, 256, 32, 16, 32
NR = N * RANK
SCALE = ALPHA / RANK


def setup_inputs():
    s, t = mx_kscale(D_IN), mx_kscale(NR)
    tn = t.reshape(N, RANK)
    return {"x": bf(np.random.standard_normal((B_, S, D_IN)) * s),
            "lora_A": bf(np.random.standard_normal((N, RANK, D_IN)) / np.sqrt(D_IN) / s * tn[:, :, None]),
            "lora_B": bf(np.random.standard_normal((N, D_OUT, RANK)) / np.sqrt(RANK) / tn[:, None, :]),
            "W": bf(np.random.standard_normal((D_OUT, D_IN)) / np.sqrt(D_IN) / s),
            "bias": bf(np.random.standard_normal(D_OUT) * 0.3),
            "lora_weights": bf((1.0 + 0.5 * np.random.standard_normal(N)) * 2.0 / N)}


def reference(x, lora_A, lora_B, W, bias, lora_weights):
    xq = mxq(f64(x), 2, "e4m3")
    h = xq @ mxq(f64(lora_A).reshape(NR, D_IN), 1, "e4m3").T
    coef = (SCALE * f64(lora_weights))[:, None, None]
    bc = (f64(lora_B) * coef).transpose(1, 0, 2).reshape(D_OUT, NR)
    lora_out = mxq(h, 2, "e4m3") @ mxq(bc, 1, "e4m3").T
    base = (xq @ mxq(f64(W), 1, "e4m3").T) + f64(bias)
    return base + lora_out

@@ -1,0 +1,224 @@
+from contextlib import ExitStack
+
+import concourse.mybir as mybir
+from concourse.masks import make_identity
+
+F32 = mybir.dt.float32
+BF16 = mybir.dt.bfloat16
+U32 = mybir.dt.uint32
+U8 = mybir.dt.uint8
+FP8X4 = mybir.dt.float8_e4m3fn_x4
+
+P = 128
+PACK = 4
+K = P * PACK
+HALVES = 2
+SUBS = 4
+TILE = SUBS * P
+LORA_SCALE = 2.0
+QUARTER = 64
+OUT_LAG = 2
+
+FLOPS = 2 * 8192 * 512 * (512 + 256 + 256)
+
+
+def tile_replaced_compose_lora_pa_t_kernel(tc, x, lora_A, lora_B, W, bias, lora_weights, out):
+    nc = tc.nc
+    x_rows = x.flatten_outer_dims()
+    out_rows = out.flatten_outer_dims()
+    a_rows = lora_A.flatten_outer_dims()
+    rank = lora_A.shape[1]
+    d_out = W.shape[0]
+    n_tiles = x_rows.shape[0] // TILE
+    assert x_rows.shape[1] == K and a_rows.shape[0] == K and d_out == 2 * P
+
+    with ExitStack() as ctx:
+        fixed = ctx.enter_context(tc.tile_pool(name="fixed", bufs=1))
+        x_pool = ctx.enter_context(tc.tile_pool(name="x_pool", bufs=n_tiles))
+        grouped_pool = ctx.enter_context(tc.tile_pool(name="grouped_pool", bufs=2))
+        codes_pool = ctx.enter_context(tc.tile_pool(name="codes_pool", bufs=OUT_LAG + 3))
+        result_pool = ctx.enter_context(tc.tile_pool(name="result_pool", bufs=4))
+        psum_t = ctx.enter_context(tc.psum_pool(name="psum_t", bufs=2))
+        psum_h = ctx.enter_context(tc.psum_pool(name="psum_h", bufs=4))
+        psum_o = ctx.enter_context(tc.psum_pool(name="psum_o", bufs=2))
+        ctx.enter_context(tc.manual_schedule())
+
+        def load_x(i):
+            x_tile = x_pool.tile([P, SUBS, K], BF16, name="x_tile")
+            nc.sync.dma_start(
+                out=x_tile[:],
+                in_=x_rows[i * TILE : (i + 1) * TILE, :].rearrange("(c s) d -> c s d", s=SUBS),
+            )
+            return x_tile
+
+        a_in = fixed.tile([P, PACK, K], BF16)
+        nc.sync.dma_start(out=a_in[:], in_=a_rows.rearrange("(c t) d -> c t d", t=PACK))
+        x_in = [load_x(i) for i in range(2)]
+        b_in = fixed.tile([P, QUARTER * rank], BF16)
+        nc.sync.dma_start(out=b_in[:], in_=lora_B.rearrange("n (oh ol) r -> (n oh) (ol r)", ol=QUARTER))
+        w_in = fixed.tile([P, 2, K], BF16)
+        nc.sync.dma_start(out=w_in[:], in_=W.rearrange("(s c) d -> c s d", c=P))
+        x_in.extend([load_x(i) for i in range(2, n_tiles)])
+
+        mix = fixed.tile([P, 1], BF16)
+        for a in range(PACK):
+            nc.scalar.dma_start(out=mix[a:P:PACK, :], in_=lora_weights.rearrange("(n one) -> n one", one=1))
+        bias_all = fixed.tile([P, d_out], BF16)
+        nc.scalar.dma_start(out=bias_all[:], in_=bias.partition_broadcast(P))
+        bias_twice = bias_all[:].unsqueeze(1).to_broadcast([P, 2, d_out])
+
+        ident = fixed.tile([P, P], F32)
+        make_identity(nc, ident[:])
+
+        def quantise(grouped, codes, scales):
+            nc.vector.quantize_mx(out=codes.bitcast(FP8X4), scales=scales, in_=grouped)
+
+        def turn_rows(rows, grouped, psum, bank_tag, leave_last_bank):
+            subs = rows.shape[1]
+            grouped_words = grouped.bitcast(F32)
+            for pair in range(subs // 2):
+                bank = psum.tile([P, HALVES, 2, P], F32, name="turn_bank", tag=bank_tag)
+                for s in range(2):
+                    words = rows[:, 2 * pair + s, :].bitcast(F32)
+                    for u in range(HALVES):
+                        nc.tensor.transpose(out=bank[:, u, s, :], in_=words[:, u : HALVES * P : HALVES], identity=ident[:])
+                leave = leave_last_bank if pair == subs // 2 - 1 else nc.scalar.copy
+                leave(
+                    out=grouped_words[:, 2 * pair * P : 2 * (pair + 1) * P, :],
+                    in_=bank[:].rearrange("p u s c -> p (s c) u"),
+                )
+
+        def weight_words(rows, psum, bank_tag, label):
+            columns = rows.shape[1] * P
+            grouped = fixed.tile([P, columns, PACK], BF16, name=label + "_grouped", align_bytes=64)
+            codes = fixed.tile([P, columns], U32, name=label + "_codes", align_bytes=64)
+            scales = fixed.tile([P, columns], U8, name=label + "_scales", align_bytes=64)
+            turn_rows(rows, grouped[:], psum, bank_tag, nc.vector.tensor_copy)
+            quantise(grouped[:].rearrange("p c t -> p (c t)"), codes[:], scales[:])
+            return codes, scales
+
+        def sort_b():
+            b_sorted = fixed.tile([P, PACK, P], F32)
+            nc.scalar.copy(
+                out=b_sorted[:].rearrange("q a (ol w) -> q a ol w", w=2),
+                in_=b_in[:].bitcast(F32).rearrange("q (ol a w) -> q a ol w", a=PACK, w=2),
+            )
+            return b_sorted
+
+        def turn_b_first(b_sorted):
+            bank = psum_o.tile([P, PACK, P], F32, name="b_bank_first", tag="out_bank")
+            for a in range(PACK):
+                nc.tensor.transpose(out=bank[:, a, :], in_=b_sorted[:, a, :], identity=ident[:])
+            b_turned = fixed.tile([P, PACK, P], F32)
+            nc.vector.tensor_copy(
+                out=b_turned[:].rearrange("v oh (n a) -> v oh n a", a=PACK),
+                in_=bank[:].rearrange("v a (n oh) -> v oh n a", oh=PACK),
+            )
+            return b_turned
+
+        def turn_b_second(b_turned):
+            bank = psum_o.tile([P, PACK, P], F32, name="b_bank_second", tag="out_bank")
+            for oh in range(PACK):
+                nc.tensor.transpose(out=bank[:, oh, :], in_=b_turned[:, oh, :], identity=ident[:])
+            b_grouped = fixed.tile([P, d_out * PACK], BF16, align_bytes=64)
+            nc.vector.tensor_scalar(
+                out=b_grouped[:],
+                in0=bank[:].bitcast(BF16).rearrange("q oh v -> q (oh v)"),
+                scalar1=mix[:, 0:1],
+                scalar2=LORA_SCALE,
+                op0=mybir.AluOpType.mult,
+                op1=mybir.AluOpType.mult,
+            )
+            codes = fixed.tile([P, d_out], U32, name="b_codes", align_bytes=64)
+            scales = fixed.tile([P, d_out], U8, name="b_scales", align_bytes=64)
+            quantise(b_grouped[:], codes[:], scales[:])
+            return codes, scales
+
+        x_mx = {}
+        h_mx = {}
+
+        def low_rank_passes(i, h_grouped):
+            x_codes, x_scales = x_mx[i]
+            for s in range(SUBS):
+                tokens = slice(s * P, (s + 1) * P)
+                bank = psum_h.tile([P, PACK, P], F32, name="h_bank", tag="h_bank")
+                for t in range(PACK):
+                    ks = slice(t * P, (t + 1) * P)
+                    nc.tensor.matmul_mx(
+                        out=bank[:, t, :],
+                        lhsT=a_codes[:, ks].bitcast(FP8X4),
+                        lhsT_scale=a_scales[:, ks],
+                        rhs=x_codes[:, tokens].bitcast(FP8X4),
+                        rhs_scale=x_scales[:, tokens],
+                        start=True,
+                        stop=True,
+                    )
+                nc.scalar.copy(out=h_grouped[:, tokens, :], in_=bank[:].rearrange("p t c -> p c t"))
+
+        def out_passes(i):
+            x_codes, x_scales = x_mx[i]
+            h_codes, h_scales = h_mx[i]
+            out_tile = out_rows[i * TILE : (i + 1) * TILE, :].rearrange("(c s) o -> c s o", s=SUBS)
+            for pair in range(SUBS // 2):
+                bank = psum_o.tile([P, 2, d_out], F32, name="out_bank", tag="out_bank")
+                for j in range(2):
+                    tokens = slice((2 * pair + j) * P, (2 * pair + j + 1) * P)
+                    nc.tensor.matmul_mx(
+                        out=bank[:, j, :],
+                        lhsT=x_codes[:, tokens].bitcast(FP8X4),
+                        lhsT_scale=x_scales[:, tokens],
+                        rhs=w_codes[:].bitcast(FP8X4),
+                        rhs_scale=w_scales[:],
+                        start=True,
+                        stop=False,
+                    )
+                    nc.tensor.matmul_mx(
+                        out=bank[:, j, :],
+                        lhsT=h_codes[:, tokens].bitcast(FP8X4),
+                        lhsT_scale=h_scales[:, tokens],
+                        rhs=b_codes[:].bitcast(FP8X4),
+                        rhs_scale=b_scales[:],
+                        start=False,
+                        stop=True,
+                    )
+                result = result_pool.tile([P, 2, d_out], F32, name="result")
+                nc.vector.tensor_tensor(out=result[:], in0=bank[:], in1=bias_twice, op=mybir.AluOpType.add)
+                nc.sync.dma_start(out=out_tile[:, 2 * pair : 2 * pair + 2, :], in_=result[:])
+
+        def step(j):
+            has_h = 0 <= j < n_tiles
+            has_x = 0 <= j + 2 < n_tiles
+            if has_h or has_x:
+                grouped = grouped_pool.tile([P, 2, TILE, PACK], BF16, name="grouped", align_bytes=64)
+                codes = codes_pool.tile([P, 2, TILE], U32, name="codes", align_bytes=64)
+                scales = codes_pool.tile([P, 2, TILE], U8, name="scales", align_bytes=64)
+            if has_h:
+                low_rank_passes(j, grouped[:, 0])
+                h_mx[j] = (codes[:, 0], scales[:, 0])
+            if has_x:
+                by_vector = j % 2 == 0 or j < OUT_LAG
+                turn_rows(
+                    x_in[j + 2], grouped[:, 1], psum_t, "x_bank", nc.vector.tensor_copy if by_vector else nc.scalar.copy
+                )
+                x_mx[j + 2] = (codes[:, 1], scales[:, 1])
+            if 0 <= j - OUT_LAG:
+                out_passes(j - OUT_LAG)
+            if has_h or has_x:
+                filled = slice(0 if has_h else 1, 2 if has_x else 1)
+                quantise(
+                    grouped[:, filled].rearrange("p g c t -> p (g c t)"),
+                    codes[:, filled].rearrange("p g c -> p (g c)"),
+                    scales[:, filled].rearrange("p g c -> p (g c)"),
+                )
+
+        a_codes, a_scales = weight_words(a_in, psum_h, "h_bank", "a")
+        step(-2)
+        step(-1)
+        b_sorted = sort_b()
+        step(0)
+        b_turned = turn_b_first(b_sorted)
+        w_codes, w_scales = weight_words(w_in, psum_o, "out_bank", "w")
+        step(1)
+        b_codes, b_scales = turn_b_second(b_turned)
+        for j in range(2, n_tiles + OUT_LAG):
+            step(j)

@@ -37,7 +37,7 @@ def tile_replaced_compose_lora_pa_t_kernel(tc, x, lora_A, lora_B, W, bias, lora_
         x_pool = ctx.enter_context(tc.tile_pool(name="x_pool", bufs=n_tiles))
         grouped_pool = ctx.enter_context(tc.tile_pool(name="grouped_pool", bufs=2))
         codes_pool = ctx.enter_context(tc.tile_pool(name="codes_pool", bufs=OUT_LAG + 3))
-        result_pool = ctx.enter_context(tc.tile_pool(name="result_pool", bufs=4))
+        result_pool = ctx.enter_context(tc.tile_pool(name="result_pool", bufs=2 * n_tiles))
         psum_t = ctx.enter_context(tc.psum_pool(name="psum_t", bufs=2))
         psum_h = ctx.enter_context(tc.psum_pool(name="psum_h", bufs=4))
         psum_o = ctx.enter_context(tc.psum_pool(name="psum_o", bufs=2))
@@ -196,10 +196,7 @@ def tile_replaced_compose_lora_pa_t_kernel(tc, x, lora_A, lora_B, W, bias, lora_
                 low_rank_passes(j, grouped[:, 0])
                 h_mx[j] = (codes[:, 0], scales[:, 0])
             if has_x:
-                by_vector = j % 2 == 0 or j < OUT_LAG
-                turn_rows(
-                    x_in[j + 2], grouped[:, 1], psum_t, "x_bank", nc.vector.tensor_copy if by_vector else nc.scalar.copy
-                )
+                turn_rows(x_in[j + 2], grouped[:, 1], psum_t, "x_bank", nc.vector.tensor_copy)
                 x_mx[j + 2] = (codes[:, 1], scales[:, 1])
             if 0 <= j - OUT_LAG:
                 out_passes(j - OUT_LAG)

@@ -17,6 +17,7 @@ SUBS = 4
 TILE = SUBS * P
 LORA_SCALE = 2.0
 QUARTER = 64
+SORTED = 2
 OUT_LAG = 2
 
 FLOPS = 2 * 8192 * 512 * (512 + 256 + 256)
@@ -35,6 +36,7 @@ def tile_replaced_compose_lora_pa_t_kernel(tc, x, lora_A, lora_B, W, bias, lora_
     with ExitStack() as ctx:
         fixed = ctx.enter_context(tc.tile_pool(name="fixed", bufs=1))
         x_pool = ctx.enter_context(tc.tile_pool(name="x_pool", bufs=n_tiles))
+        sorted_pool = ctx.enter_context(tc.tile_pool(name="sorted_pool", bufs=2))
         grouped_pool = ctx.enter_context(tc.tile_pool(name="grouped_pool", bufs=2))
         codes_pool = ctx.enter_context(tc.tile_pool(name="codes_pool", bufs=OUT_LAG + 3))
         result_pool = ctx.enter_context(tc.tile_pool(name="result_pool", bufs=2 * n_tiles))
@@ -73,29 +75,42 @@ def tile_replaced_compose_lora_pa_t_kernel(tc, x, lora_A, lora_B, W, bias, lora_
         def quantise(grouped, codes, scales):
             nc.vector.quantize_mx(out=codes.bitcast(FP8X4), scales=scales, in_=grouped)
 
-        def turn_rows(rows, grouped, psum, bank_tag, leave_last_bank):
-            subs = rows.shape[1]
+        def turn_rows(words_of, grouped, psum, bank_tag, leave_last_bank):
+            subs = grouped.shape[1] // P
             grouped_words = grouped.bitcast(F32)
             for pair in range(subs // 2):
                 bank = psum.tile([P, HALVES, 2, P], F32, name="turn_bank", tag=bank_tag)
                 for s in range(2):
-                    words = rows[:, 2 * pair + s, :].bitcast(F32)
                     for u in range(HALVES):
-                        nc.tensor.transpose(out=bank[:, u, s, :], in_=words[:, u : HALVES * P : HALVES], identity=ident[:])
+                        nc.tensor.transpose(out=bank[:, u, s, :], in_=words_of(2 * pair + s, u), identity=ident[:])
                 leave = leave_last_bank if pair == subs // 2 - 1 else nc.scalar.copy
                 leave(
                     out=grouped_words[:, 2 * pair * P : 2 * (pair + 1) * P, :],
                     in_=bank[:].rearrange("p u s c -> p (s c) u"),
                 )
 
+        def as_loaded(rows):
+            return lambda s, u: rows[:, s, :].bitcast(F32)[:, u : HALVES * P : HALVES]
+
+        def sort_x(i):
+            x_sorted = sorted_pool.tile([P, SORTED, HALVES, P], F32, name="x_sorted")
+            nc.vector.tensor_copy(
+                out=x_sorted[:].rearrange("c s u p -> c s p u"),
+                in_=x_in[i][:, SUBS - SORTED :, :]
+                .rearrange("c s d -> c (s d)")
+                .bitcast(F32)
+                .rearrange("c (s p u) -> c s p u", s=SORTED, u=HALVES),
+            )
+            loaded = as_loaded(x_in[i])
+            return lambda s, u: x_sorted[:, s - (SUBS - SORTED), u, :] if s >= SUBS - SORTED else loaded(s, u)
+
         def weight_words(rows, psum, bank_tag, label):
             columns = rows.shape[1] * P
             grouped = fixed.tile([P, columns, PACK], BF16, name=label + "_grouped", align_bytes=64)
             codes = fixed.tile([P, columns], U32, name=label + "_codes", align_bytes=64)
             scales = fixed.tile([P, columns], U8, name=label + "_scales", align_bytes=64)
-            turn_rows(rows, grouped[:], psum, bank_tag, nc.vector.tensor_copy)
-            quantise(grouped[:].rearrange("p c t -> p (c t)"), codes[:], scales[:])
-            return codes, scales
+            turn_rows(as_loaded(rows), grouped[:], psum, bank_tag, nc.vector.tensor_copy)
+            return codes, scales, lambda: quantise(grouped[:].rearrange("p c t -> p (c t)"), codes[:], scales[:])
 
         def sort_b():
             b_sorted = fixed.tile([P, PACK, P], F32)
@@ -134,6 +149,7 @@ def tile_replaced_compose_lora_pa_t_kernel(tc, x, lora_A, lora_B, W, bias, lora_
             quantise(b_grouped[:], codes[:], scales[:])
             return codes, scales
 
+        x_words = {i: as_loaded(x_in[i]) for i in range(n_tiles)}
         x_mx = {}
         h_mx = {}
 
@@ -185,9 +201,11 @@ def tile_replaced_compose_lora_pa_t_kernel(tc, x, lora_A, lora_B, W, bias, lora_
                 nc.vector.tensor_tensor(out=result[:], in0=bank[:], in1=bias_twice, op=mybir.AluOpType.add)
                 nc.sync.dma_start(out=out_tile[:, 2 * pair : 2 * pair + 2, :], in_=result[:])
 
-        def step(j):
+        def step(j, before_quantising=None):
             has_h = 0 <= j < n_tiles
             has_x = 0 <= j + 2 < n_tiles
+            if 0 < j < n_tiles - 3:
+                x_words[j + 3] = sort_x(j + 3)
             if has_h or has_x:
                 grouped = grouped_pool.tile([P, 2, TILE, PACK], BF16, name="grouped", align_bytes=64)
                 codes = codes_pool.tile([P, 2, TILE], U32, name="codes", align_bytes=64)
@@ -196,10 +214,12 @@ def tile_replaced_compose_lora_pa_t_kernel(tc, x, lora_A, lora_B, W, bias, lora_
                 low_rank_passes(j, grouped[:, 0])
                 h_mx[j] = (codes[:, 0], scales[:, 0])
             if has_x:
-                turn_rows(x_in[j + 2], grouped[:, 1], psum_t, "x_bank", nc.vector.tensor_copy)
+                turn_rows(x_words[j + 2], grouped[:, 1], psum_t, "x_bank", nc.vector.tensor_copy)
                 x_mx[j + 2] = (codes[:, 1], scales[:, 1])
             if 0 <= j - OUT_LAG:
                 out_passes(j - OUT_LAG)
+            if before_quantising:
+                before_quantising()
             if has_h or has_x:
                 filled = slice(0 if has_h else 1, 2 if has_x else 1)
                 quantise(
@@ -208,14 +228,24 @@ def tile_replaced_compose_lora_pa_t_kernel(tc, x, lora_A, lora_B, W, bias, lora_
                     scales[:, filled].rearrange("p g c -> p (g c)"),
                 )
 
-        a_codes, a_scales = weight_words(a_in, psum_h, "h_bank", "a")
+        a_codes, a_scales, quantise_a = weight_words(a_in, psum_h, "h_bank", "a")
+        quantise_a()
         step(-2)
         step(-1)
         b_sorted = sort_b()
-        step(0)
-        b_turned = turn_b_first(b_sorted)
-        w_codes, w_scales = weight_words(w_in, psum_o, "out_bank", "w")
-        step(1)
-        b_codes, b_scales = turn_b_second(b_turned)
+        weights = {}
+
+        def first_turns():
+            weights["b_turned"] = turn_b_first(b_sorted)
+            weights["w"] = weight_words(w_in, psum_o, "out_bank", "w")
+
+        def second_turn():
+            weights["b"] = turn_b_second(weights["b_turned"])
+
+        step(0, first_turns)
+        w_codes, w_scales, quantise_w = weights["w"]
+        quantise_w()
+        step(1, second_turn)
+        b_codes, b_scales = weights["b"]
         for j in range(2, n_tiles + OUT_LAG):
             step(j)

@@ -75,7 +75,15 @@ def tile_replaced_compose_lora_pa_t_kernel(tc, x, lora_A, lora_B, W, bias, lora_
         def quantise(grouped, codes, scales):
             nc.vector.quantize_mx(out=codes.bitcast(FP8X4), scales=scales, in_=grouped)
 
-        def turn_rows(words_of, grouped, psum, bank_tag, leave_last_bank):
+        warm_in = fixed.tile([P, K], BF16)
+        nc.vector.memset(warm_in[:], 0.0)
+        warm_bank = psum_h.tile([P, K], F32, name="warm_bank", tag="h_bank")
+
+        def keep_warm(count):
+            for turn in range(count):
+                nc.tensor.matmul(out=warm_bank[:], lhsT=warm_in[:, :P], rhs=warm_in[:], start=True, stop=True)
+
+        def turn_rows(words_of, grouped, psum, bank_tag, leave_last_bank, warm=0):
             subs = grouped.shape[1] // P
             grouped_words = grouped.bitcast(F32)
             for pair in range(subs // 2):
@@ -83,6 +91,7 @@ def tile_replaced_compose_lora_pa_t_kernel(tc, x, lora_A, lora_B, W, bias, lora_
                 for s in range(2):
                     for u in range(HALVES):
                         nc.tensor.transpose(out=bank[:, u, s, :], in_=words_of(2 * pair + s, u), identity=ident[:])
+                keep_warm(warm)
                 leave = leave_last_bank if pair == subs // 2 - 1 else nc.scalar.copy
                 leave(
                     out=grouped_words[:, 2 * pair * P : 2 * (pair + 1) * P, :],
@@ -104,12 +113,12 @@ def tile_replaced_compose_lora_pa_t_kernel(tc, x, lora_A, lora_B, W, bias, lora_
             loaded = as_loaded(x_in[i])
             return lambda s, u: x_sorted[:, s - (SUBS - SORTED), u, :] if s >= SUBS - SORTED else loaded(s, u)
 
-        def weight_words(rows, psum, bank_tag, label):
+        def weight_words(rows, psum, bank_tag, label, warm=0):
             columns = rows.shape[1] * P
             grouped = fixed.tile([P, columns, PACK], BF16, name=label + "_grouped", align_bytes=64)
             codes = fixed.tile([P, columns], U32, name=label + "_codes", align_bytes=64)
             scales = fixed.tile([P, columns], U8, name=label + "_scales", align_bytes=64)
-            turn_rows(as_loaded(rows), grouped[:], psum, bank_tag, nc.vector.tensor_copy)
+            turn_rows(as_loaded(rows), grouped[:], psum, bank_tag, nc.vector.tensor_copy, warm)
             return codes, scales, lambda: quantise(grouped[:].rearrange("p c t -> p (c t)"), codes[:], scales[:])
 
         def sort_b():
@@ -214,7 +223,13 @@ def tile_replaced_compose_lora_pa_t_kernel(tc, x, lora_A, lora_B, W, bias, lora_
                 low_rank_passes(j, grouped[:, 0])
                 h_mx[j] = (codes[:, 0], scales[:, 0])
             if has_x:
-                turn_rows(x_words[j + 2], grouped[:, 1], psum_t, "x_bank", nc.vector.tensor_copy)
+                turn_rows(
+                    x_words[j + 2],
+                    grouped[:, 1],
+                    *((psum_o, "out_bank") if j == -1 else (psum_t, "x_bank")),
+                    nc.scalar.copy if j == -2 else nc.vector.tensor_copy,
+                    warm=1 if j < 0 else 0,
+                )
                 x_mx[j + 2] = (codes[:, 1], scales[:, 1])
             if 0 <= j - OUT_LAG:
                 out_passes(j - OUT_LAG)
@@ -228,7 +243,8 @@ def tile_replaced_compose_lora_pa_t_kernel(tc, x, lora_A, lora_B, W, bias, lora_
                     scales[:, filled].rearrange("p g c -> p (g c)"),
                 )
 
-        a_codes, a_scales, quantise_a = weight_words(a_in, psum_h, "h_bank", "a")
+        keep_warm(5)
+        a_codes, a_scales, quantise_a = weight_words(a_in, psum_h, "h_bank", "a", warm=1)
         quantise_a()
         step(-2)
         step(-1)

@@ -62,12 +62,33 @@ def tile_replaced_compose_lora_pa_t_kernel(tc, x, lora_A, lora_B, W, bias, lora_
         nc.sync.dma_start(out=w_in[:], in_=W.rearrange("(s c) d -> c s d", c=P))
         x_in.extend([load_x(i) for i in range(2, n_tiles)])
 
-        mix = fixed.tile([P, 1], BF16)
-        for a in range(PACK):
-            nc.scalar.dma_start(out=mix[a:P:PACK, :], in_=lora_weights.rearrange("(n one) -> n one", one=1))
-        bias_all = fixed.tile([P, d_out], BF16)
-        nc.scalar.dma_start(out=bias_all[:], in_=bias.partition_broadcast(P))
+        n_adapters = lora_weights.shape[0]
+        rows = fixed.tile([P, d_out + n_adapters], BF16, name="rows")
+        nc.vector.memset(rows[:], 0.0)
+        nc.scalar.dma_start(out=rows[0:1, :d_out], in_=bias.rearrange("(one o) -> one o", one=1))
+        nc.scalar.dma_start(out=rows[0:1, d_out:], in_=lora_weights.rearrange("(one n) -> one n", one=1))
+        ones = fixed.tile([P, P], BF16, name="ones")
+        nc.vector.memset(ones[:], 1.0)
+        bias_all = fixed.tile([P, d_out], F32, name="bias_all")
         bias_twice = bias_all[:].unsqueeze(1).to_broadcast([P, 2, d_out])
+        mix = fixed.tile([P, 1], F32, name="mix")
+
+        def spread_vectors():
+            mix_row = fixed.tile([P, n_adapters, PACK], BF16, name="mix_row")
+            nc.vector.tensor_copy(
+                out=mix_row[:], in_=rows[:, d_out:].unsqueeze(2).to_broadcast([P, n_adapters, PACK])
+            )
+            bank = psum_h.tile([P, d_out + 1], F32, name="vector_bank", tag="h_bank")
+            nc.tensor.matmul(out=bank[:, :d_out], lhsT=ones[:], rhs=rows[:, :d_out], start=True, stop=True)
+            nc.tensor.matmul(
+                out=bank[:, d_out:],
+                lhsT=mix_row[:].rearrange("p n a -> p (n a)"),
+                rhs=ones[:, 0:1],
+                start=True,
+                stop=True,
+            )
+            nc.scalar.copy(out=bias_all[:], in_=bank[:, :d_out])
+            nc.scalar.copy(out=mix[:], in_=bank[:, d_out:])
 
         ident = fixed.tile([P, P], F32)
         make_identity(nc, ident[:])
@@ -247,6 +268,7 @@ def tile_replaced_compose_lora_pa_t_kernel(tc, x, lora_A, lora_B, W, bias, lora_
         a_codes, a_scales, quantise_a = weight_words(a_in, psum_h, "h_bank", "a", warm=1)
         quantise_a()
         step(-2)
+        spread_vectors()
         step(-1)
         b_sorted = sort_b()
         weights = {}

@@ -45,6 +45,9 @@ def tile_replaced_compose_lora_pa_t_kernel(tc, x, lora_A, lora_B, W, bias, lora_
         psum_o = ctx.enter_context(tc.psum_pool(name="psum_o", bufs=2))
         ctx.enter_context(tc.manual_schedule())
 
+        ident = fixed.tile([P, P], F32)
+        make_identity(nc, ident[:])
+
         def load_x(i):
             x_tile = x_pool.tile([P, SUBS, K], BF16, name="x_tile")
             nc.sync.dma_start(
@@ -60,25 +63,22 @@ def tile_replaced_compose_lora_pa_t_kernel(tc, x, lora_A, lora_B, W, bias, lora_
         nc.sync.dma_start(out=b_in[:], in_=lora_B.rearrange("n (oh ol) r -> (n oh) (ol r)", ol=QUARTER))
         w_in = fixed.tile([P, 2, K], BF16)
         nc.sync.dma_start(out=w_in[:], in_=W.rearrange("(s c) d -> c s d", c=P))
-        x_in.extend([load_x(i) for i in range(2, n_tiles)])
-
         n_adapters = lora_weights.shape[0]
         rows = fixed.tile([P, d_out + n_adapters], BF16, name="rows")
-        nc.vector.memset(rows[:], 0.0)
-        nc.scalar.dma_start(out=rows[0:1, :d_out], in_=bias.rearrange("(one o) -> one o", one=1))
-        nc.scalar.dma_start(out=rows[0:1, d_out:], in_=lora_weights.rearrange("(one n) -> one n", one=1))
+        nc.gpsimd.memset(rows[:], 0.0)
+        nc.sync.dma_start(out=rows[0:1, :d_out], in_=bias.rearrange("(one o) -> one o", one=1))
+        nc.sync.dma_start(out=rows[0:1, d_out:], in_=lora_weights.rearrange("(one n) -> one n", one=1))
         ones = fixed.tile([P, P], BF16, name="ones")
-        nc.vector.memset(ones[:], 1.0)
+        nc.gpsimd.memset(ones[:], 1.0)
+        x_in.extend([load_x(i) for i in range(2, n_tiles)])
+
         bias_all = fixed.tile([P, d_out], F32, name="bias_all")
         bias_twice = bias_all[:].unsqueeze(1).to_broadcast([P, 2, d_out])
         mix = fixed.tile([P, 1], F32, name="mix")
+        mix_row = fixed.tile([P, n_adapters, PACK], BF16, name="mix_row")
 
         def spread_vectors():
-            mix_row = fixed.tile([P, n_adapters, PACK], BF16, name="mix_row")
-            nc.vector.tensor_copy(
-                out=mix_row[:], in_=rows[:, d_out:].unsqueeze(2).to_broadcast([P, n_adapters, PACK])
-            )
-            bank = psum_h.tile([P, d_out + 1], F32, name="vector_bank", tag="h_bank")
+            bank = psum_o.tile([P, d_out + 1], F32, name="vector_bank", tag="out_bank")
             nc.tensor.matmul(out=bank[:, :d_out], lhsT=ones[:], rhs=rows[:, :d_out], start=True, stop=True)
             nc.tensor.matmul(
                 out=bank[:, d_out:],
@@ -87,11 +87,8 @@ def tile_replaced_compose_lora_pa_t_kernel(tc, x, lora_A, lora_B, W, bias, lora_
                 start=True,
                 stop=True,
             )
+            nc.vector.tensor_copy(out=mix[:], in_=bank[:, d_out:])
             nc.scalar.copy(out=bias_all[:], in_=bank[:, :d_out])
-            nc.scalar.copy(out=mix[:], in_=bank[:, d_out:])
-
-        ident = fixed.tile([P, P], F32)
-        make_identity(nc, ident[:])
 
         def quantise(grouped, codes, scales):
             nc.vector.quantize_mx(out=codes.bitcast(FP8X4), scales=scales, in_=grouped)
@@ -206,7 +203,10 @@ def tile_replaced_compose_lora_pa_t_kernel(tc, x, lora_A, lora_B, W, bias, lora_
             h_codes, h_scales = h_mx[i]
             out_tile = out_rows[i * TILE : (i + 1) * TILE, :].rearrange("(c s) o -> c s o", s=SUBS)
             for pair in range(SUBS // 2):
-                bank = psum_o.tile([P, 2, d_out], F32, name="out_bank", tag="out_bank")
+                free = pair == 1 and i >= n_tiles - OUT_LAG - 2
+                bank = (psum_t if free else psum_o).tile(
+                    [P, 2, d_out], F32, name="out_bank", tag="x_bank" if free else "out_bank"
+                )
                 for j in range(2):
                     tokens = slice((2 * pair + j) * P, (2 * pair + j + 1) * P)
                     nc.tensor.matmul_mx(
@@ -268,7 +268,6 @@ def tile_replaced_compose_lora_pa_t_kernel(tc, x, lora_A, lora_B, W, bias, lora_
         a_codes, a_scales, quantise_a = weight_words(a_in, psum_h, "h_bank", "a", warm=1)
         quantise_a()
         step(-2)
-        spread_vectors()
         step(-1)
         b_sorted = sort_b()
         weights = {}
@@ -276,8 +275,10 @@ def tile_replaced_compose_lora_pa_t_kernel(tc, x, lora_A, lora_B, W, bias, lora_
         def first_turns():
             weights["b_turned"] = turn_b_first(b_sorted)
             weights["w"] = weight_words(w_in, psum_o, "out_bank", "w")
+            nc.vector.tensor_copy(out=mix_row[:], in_=rows[:, d_out:].unsqueeze(2).to_broadcast([P, n_adapters, PACK]))
 
         def second_turn():
+            spread_vectors()
             weights["b"] = turn_b_second(weights["b_turned"])
 
         step(0, first_turns)

@@ -17,7 +17,7 @@ SUBS = 4
 TILE = SUBS * P
 LORA_SCALE = 2.0
 QUARTER = 64
-SORTED = 2
+SORTED = 3
 OUT_LAG = 2
 
 FLOPS = 2 * 8192 * 512 * (512 + 256 + 256)
@@ -39,7 +39,7 @@ def tile_replaced_compose_lora_pa_t_kernel(tc, x, lora_A, lora_B, W, bias, lora_
         sorted_pool = ctx.enter_context(tc.tile_pool(name="sorted_pool", bufs=2))
         grouped_pool = ctx.enter_context(tc.tile_pool(name="grouped_pool", bufs=2))
         codes_pool = ctx.enter_context(tc.tile_pool(name="codes_pool", bufs=OUT_LAG + 3))
-        result_pool = ctx.enter_context(tc.tile_pool(name="result_pool", bufs=2 * n_tiles))
+        result_pool = ctx.enter_context(tc.tile_pool(name="result_pool", bufs=2 * n_tiles + 1))
         psum_t = ctx.enter_context(tc.psum_pool(name="psum_t", bufs=2))
         psum_h = ctx.enter_context(tc.psum_pool(name="psum_h", bufs=4))
         psum_o = ctx.enter_context(tc.psum_pool(name="psum_o", bufs=2))
@@ -56,9 +56,14 @@ def tile_replaced_compose_lora_pa_t_kernel(tc, x, lora_A, lora_B, W, bias, lora_
             )
             return x_tile
 
+        x_first = x_pool.tile([P, SUBS, K], BF16, name="x_tile")
         a_in = fixed.tile([P, PACK, K], BF16)
-        nc.sync.dma_start(out=a_in[:], in_=a_rows.rearrange("(c t) d -> c t d", t=PACK))
-        x_in = [load_x(i) for i in range(2)]
+        for half in (slice(0, 2), slice(2, 4)):
+            nc.sync.dma_start(
+                out=x_first[:, half, :], in_=x_rows[:TILE, :].rearrange("(c s) d -> c s d", s=SUBS)[:, half, :]
+            )
+            nc.sync.dma_start(out=a_in[:, half, :], in_=a_rows.rearrange("(c t) d -> c t d", t=PACK)[:, half, :])
+        x_in = [x_first, load_x(1)]
         b_in = fixed.tile([P, QUARTER * rank], BF16)
         nc.sync.dma_start(out=b_in[:], in_=lora_B.rearrange("n (oh ol) r -> (n oh) (ol r)", ol=QUARTER))
         w_in = fixed.tile([P, 2, K], BF16)
@@ -101,43 +106,42 @@ def tile_replaced_compose_lora_pa_t_kernel(tc, x, lora_A, lora_B, W, bias, lora_
             for turn in range(count):
                 nc.tensor.matmul(out=warm_bank[:], lhsT=warm_in[:, :P], rhs=warm_in[:], start=True, stop=True)
 
-        def turn_rows(words_of, grouped, psum, bank_tag, leave_last_bank, warm=0):
-            subs = grouped.shape[1] // P
-            grouped_words = grouped.bitcast(F32)
-            for pair in range(subs // 2):
-                bank = psum.tile([P, HALVES, 2, P], F32, name="turn_bank", tag=bank_tag)
-                for s in range(2):
-                    for u in range(HALVES):
-                        nc.tensor.transpose(out=bank[:, u, s, :], in_=words_of(2 * pair + s, u), identity=ident[:])
-                keep_warm(warm)
-                leave = leave_last_bank if pair == subs // 2 - 1 else nc.scalar.copy
-                leave(
-                    out=grouped_words[:, 2 * pair * P : 2 * (pair + 1) * P, :],
-                    in_=bank[:].rearrange("p u s c -> p (s c) u"),
-                )
+        def turn_bank(words_of, pair, grouped, psum, bank_tag, leave, warm=0):
+            bank = psum.tile([P, HALVES, 2, P], F32, name="turn_bank", tag=bank_tag)
+            for s in range(2):
+                for u in range(HALVES):
+                    nc.tensor.transpose(out=bank[:, u, s, :], in_=words_of(2 * pair + s, u), identity=ident[:])
+            keep_warm(warm)
+            leave(
+                out=grouped.bitcast(F32)[:, 2 * pair * P : 2 * (pair + 1) * P, :],
+                in_=bank[:].rearrange("p u s c -> p (s c) u"),
+            )
 
         def as_loaded(rows):
             return lambda s, u: rows[:, s, :].bitcast(F32)[:, u : HALVES * P : HALVES]
 
         def sort_x(i):
             x_sorted = sorted_pool.tile([P, SORTED, HALVES, P], F32, name="x_sorted")
-            nc.vector.tensor_copy(
-                out=x_sorted[:].rearrange("c s u p -> c s p u"),
-                in_=x_in[i][:, SUBS - SORTED :, :]
-                .rearrange("c s d -> c (s d)")
-                .bitcast(F32)
-                .rearrange("c (s p u) -> c s p u", s=SORTED, u=HALVES),
-            )
+            for part in (slice(0, 1), slice(1, 3)):
+                loaded_part = x_in[i][:, SUBS - SORTED :, :][:, part, :]
+                nc.vector.tensor_copy(
+                    out=x_sorted[:, part].rearrange("c s u p -> c s p u"),
+                    in_=loaded_part.rearrange("c s d -> c (s d)")
+                    .bitcast(F32)
+                    .rearrange("c (s p u) -> c s p u", s=loaded_part.shape[1], u=HALVES),
+                )
             loaded = as_loaded(x_in[i])
             return lambda s, u: x_sorted[:, s - (SUBS - SORTED), u, :] if s >= SUBS - SORTED else loaded(s, u)
 
-        def weight_words(rows, psum, bank_tag, label, warm=0):
-            columns = rows.shape[1] * P
+        def weight_tiles(label, columns):
             grouped = fixed.tile([P, columns, PACK], BF16, name=label + "_grouped", align_bytes=64)
             codes = fixed.tile([P, columns], U32, name=label + "_codes", align_bytes=64)
             scales = fixed.tile([P, columns], U8, name=label + "_scales", align_bytes=64)
-            turn_rows(as_loaded(rows), grouped[:], psum, bank_tag, nc.vector.tensor_copy, warm)
-            return codes, scales, lambda: quantise(grouped[:].rearrange("p c t -> p (c t)"), codes[:], scales[:])
+            return grouped[:], codes[:], scales[:]
+
+        def quantise_columns(tiles, columns):
+            grouped, codes, scales = tiles
+            quantise(grouped[:, columns, :].rearrange("p c t -> p (c t)"), codes[:, columns], scales[:, columns])
 
         def sort_b():
             b_sorted = fixed.tile([P, PACK, P], F32)
@@ -202,15 +206,16 @@ def tile_replaced_compose_lora_pa_t_kernel(tc, x, lora_A, lora_B, W, bias, lora_
             x_codes, x_scales = x_mx[i]
             h_codes, h_scales = h_mx[i]
             out_tile = out_rows[i * TILE : (i + 1) * TILE, :].rearrange("(c s) o -> c s o", s=SUBS)
-            for pair in range(SUBS // 2):
-                free = pair == 1 and i >= n_tiles - OUT_LAG - 2
+            splits = ((0, 2), (2, 3), (3, 4)) if i == n_tiles - 1 else ((0, 2), (2, 4))
+            for number, (first, end) in enumerate(splits):
+                free = number == 1 and i >= n_tiles - OUT_LAG - 2
                 bank = (psum_t if free else psum_o).tile(
-                    [P, 2, d_out], F32, name="out_bank", tag="x_bank" if free else "out_bank"
+                    [P, end - first, d_out], F32, name="out_bank", tag="x_bank" if free else "out_bank"
                 )
-                for j in range(2):
-                    tokens = slice((2 * pair + j) * P, (2 * pair + j + 1) * P)
+                for s in range(first, end):
+                    tokens = slice(s * P, (s + 1) * P)
                     nc.tensor.matmul_mx(
-                        out=bank[:, j, :],
+                        out=bank[:, s - first, :],
                         lhsT=x_codes[:, tokens].bitcast(FP8X4),
                         lhsT_scale=x_scales[:, tokens],
                         rhs=w_codes[:].bitcast(FP8X4),
@@ -219,7 +224,7 @@ def tile_replaced_compose_lora_pa_t_kernel(tc, x, lora_A, lora_B, W, bias, lora_
                         stop=False,
                     )
                     nc.tensor.matmul_mx(
-                        out=bank[:, j, :],
+                        out=bank[:, s - first, :],
                         lhsT=h_codes[:, tokens].bitcast(FP8X4),
                         lhsT_scale=h_scales[:, tokens],
                         rhs=b_codes[:].bitcast(FP8X4),
@@ -227,9 +232,17 @@ def tile_replaced_compose_lora_pa_t_kernel(tc, x, lora_A, lora_B, W, bias, lora_
                         start=False,
                         stop=True,
                     )
-                result = result_pool.tile([P, 2, d_out], F32, name="result")
-                nc.vector.tensor_tensor(out=result[:], in0=bank[:], in1=bias_twice, op=mybir.AluOpType.add)
-                nc.sync.dma_start(out=out_tile[:, 2 * pair : 2 * pair + 2, :], in_=result[:])
+                result = result_pool.tile([P, end - first, d_out], F32, name="result")
+                nc.vector.tensor_tensor(
+                    out=result[:], in0=bank[:], in1=bias_twice[:, : end - first, :], op=mybir.AluOpType.add
+                )
+                nc.sync.dma_start(out=out_tile[:, first:end, :], in_=result[:])
+
+        def step_tiles():
+            grouped = grouped_pool.tile([P, 2, TILE, PACK], BF16, name="grouped", align_bytes=64)
+            codes = codes_pool.tile([P, 2, TILE], U32, name="codes", align_bytes=64)
+            scales = codes_pool.tile([P, 2, TILE], U8, name="scales", align_bytes=64)
+            return grouped, codes, scales
 
         def step(j, before_quantising=None):
             has_h = 0 <= j < n_tiles
@@ -237,20 +250,16 @@ def tile_replaced_compose_lora_pa_t_kernel(tc, x, lora_A, lora_B, W, bias, lora_
             if 0 < j < n_tiles - 3:
                 x_words[j + 3] = sort_x(j + 3)
             if has_h or has_x:
-                grouped = grouped_pool.tile([P, 2, TILE, PACK], BF16, name="grouped", align_bytes=64)
-                codes = codes_pool.tile([P, 2, TILE], U32, name="codes", align_bytes=64)
-                scales = codes_pool.tile([P, 2, TILE], U8, name="scales", align_bytes=64)
+                grouped, codes, scales = step_tiles()
             if has_h:
                 low_rank_passes(j, grouped[:, 0])
                 h_mx[j] = (codes[:, 0], scales[:, 0])
             if has_x:
-                turn_rows(
-                    x_words[j + 2],
-                    grouped[:, 1],
-                    *((psum_o, "out_bank") if j == -1 else (psum_t, "x_bank")),
-                    nc.scalar.copy if j == -2 else nc.vector.tensor_copy,
-                    warm=1 if j < 0 else 0,
-                )
+                place = (psum_o, "out_bank") if j < 0 else (psum_t, "x_bank")
+                warm = 1 if j < 0 else 0
+                by_turns = nc.scalar.copy if j > 0 and j % 3 == 2 else nc.vector.tensor_copy
+                turn_bank(x_words[j + 2], 0, grouped[:, 1], *place, nc.scalar.copy, warm)
+                turn_bank(x_words[j + 2], 1, grouped[:, 1], *place, by_turns, warm)
                 x_mx[j + 2] = (codes[:, 1], scales[:, 1])
             if 0 <= j - OUT_LAG:
                 out_passes(j - OUT_LAG)
@@ -264,17 +273,30 @@ def tile_replaced_compose_lora_pa_t_kernel(tc, x, lora_A, lora_B, W, bias, lora_
                     scales[:, filled].rearrange("p g c -> p (g c)"),
                 )
 
-        keep_warm(5)
-        a_codes, a_scales, quantise_a = weight_words(a_in, psum_h, "h_bank", "a", warm=1)
-        quantise_a()
-        step(-2)
+        grouped, codes, scales = step_tiles()
+        x_mx[0] = (codes[:, 1], scales[:, 1])
+        x_tiles = (grouped[:, 1], codes[:, 1], scales[:, 1])
+        a_tiles = weight_tiles("a", K)
+        a_codes, a_scales = a_tiles[1:]
+        halves = (slice(0, 2 * P), slice(2 * P, 4 * P))
+        keep_warm(4)
+        turn_bank(x_words[0], 0, x_tiles[0], psum_t, "x_bank", nc.vector.tensor_copy, warm=1)
+        turn_bank(as_loaded(a_in), 0, a_tiles[0], psum_h, "h_bank", nc.scalar.copy, warm=1)
+        quantise_columns(x_tiles, halves[0])
+        turn_bank(x_words[0], 1, x_tiles[0], psum_t, "x_bank", nc.vector.tensor_copy, warm=1)
+        turn_bank(as_loaded(a_in), 1, a_tiles[0], psum_h, "h_bank", nc.scalar.copy, warm=1)
+        quantise_columns(a_tiles, halves[0])
+        quantise_columns(x_tiles, halves[1])
+        quantise_columns(a_tiles, halves[1])
         step(-1)
         b_sorted = sort_b()
         weights = {}
+        w_tiles = weight_tiles("w", d_out)
+        w_codes, w_scales = w_tiles[1:]
 
         def first_turns():
             weights["b_turned"] = turn_b_first(b_sorted)
-            weights["w"] = weight_words(w_in, psum_o, "out_bank", "w")
+            turn_bank(as_loaded(w_in), 0, w_tiles[0], psum_o, "out_bank", nc.vector.tensor_copy)
             nc.vector.tensor_copy(out=mix_row[:], in_=rows[:, d_out:].unsqueeze(2).to_broadcast([P, n_adapters, PACK]))
 
         def second_turn():
@@ -282,8 +304,7 @@ def tile_replaced_compose_lora_pa_t_kernel(tc, x, lora_A, lora_B, W, bias, lora_
             weights["b"] = turn_b_second(weights["b_turned"])
 
         step(0, first_turns)
-        w_codes, w_scales, quantise_w = weights["w"]
-        quantise_w()
+        quantise_columns(w_tiles, slice(0, d_out))
         step(1, second_turn)
         b_codes, b_scales = weights["b"]
         for j in range(2, n_tiles + OUT_LAG):

@@ -17,7 +17,7 @@ SUBS = 4
 TILE = SUBS * P
 LORA_SCALE = 2.0
 QUARTER = 64
-SORTED = 3
+SORTED = 2
 OUT_LAG = 2
 
 FLOPS = 2 * 8192 * 512 * (512 + 256 + 256)
@@ -98,13 +98,14 @@ def tile_replaced_compose_lora_pa_t_kernel(tc, x, lora_A, lora_B, W, bias, lora_
         def quantise(grouped, codes, scales):
             nc.vector.quantize_mx(out=codes.bitcast(FP8X4), scales=scales, in_=grouped)
 
-        warm_in = fixed.tile([P, K], BF16)
-        nc.vector.memset(warm_in[:], 0.0)
+        zeros = fixed.tile([P, K // 2], F32, name="zeros")
+        nc.vector.memset(zeros[:], 0.0)
+        warm_in = zeros[:].bitcast(BF16)
         warm_bank = psum_h.tile([P, K], F32, name="warm_bank", tag="h_bank")
 
         def keep_warm(count):
             for turn in range(count):
-                nc.tensor.matmul(out=warm_bank[:], lhsT=warm_in[:, :P], rhs=warm_in[:], start=True, stop=True)
+                nc.tensor.matmul(out=warm_bank[:], lhsT=warm_in[:, :P], rhs=warm_in, start=True, stop=True)
 
         def turn_bank(words_of, pair, grouped, psum, bank_tag, leave, warm=0):
             bank = psum.tile([P, HALVES, 2, P], F32, name="turn_bank", tag=bank_tag)
@@ -122,16 +123,30 @@ def tile_replaced_compose_lora_pa_t_kernel(tc, x, lora_A, lora_B, W, bias, lora_
 
         def sort_x(i):
             x_sorted = sorted_pool.tile([P, SORTED, HALVES, P], F32, name="x_sorted")
-            for part in (slice(0, 1), slice(1, 3)):
-                loaded_part = x_in[i][:, SUBS - SORTED :, :][:, part, :]
-                nc.vector.tensor_copy(
-                    out=x_sorted[:, part].rearrange("c s u p -> c s p u"),
-                    in_=loaded_part.rearrange("c s d -> c (s d)")
-                    .bitcast(F32)
-                    .rearrange("c (s p u) -> c s p u", s=loaded_part.shape[1], u=HALVES),
+            nc.vector.tensor_copy(
+                out=x_sorted[:].rearrange("c s u p -> c s p u"),
+                in_=x_in[i][:, SUBS - SORTED :, :]
+                .rearrange("c s d -> c (s d)")
+                .bitcast(F32)
+                .rearrange("c (s p u) -> c s p u", s=SORTED, u=HALVES),
+            )
+            x_pairs = sorted_pool.tile([P, SUBS - SORTED, HALVES, 2 * P], BF16, name="x_pairs")
+            for s in range(SUBS - SORTED):
+                nc.gpsimd.tensor_scalar(
+                    out=x_pairs[:, s].rearrange("c u (p e) -> c u p e", e=2),
+                    in0=x_in[i][:, s, :].rearrange("c (p u e) -> c u p e", u=HALVES, e=2),
+                    scalar1=1.0,
+                    scalar2=0.0,
+                    op0=mybir.AluOpType.mult,
+                    op1=mybir.AluOpType.add,
                 )
-            loaded = as_loaded(x_in[i])
-            return lambda s, u: x_sorted[:, s - (SUBS - SORTED), u, :] if s >= SUBS - SORTED else loaded(s, u)
+
+            def words_of(s, u):
+                if s >= SUBS - SORTED:
+                    return x_sorted[:, s - (SUBS - SORTED), u, :]
+                return x_pairs[:, s, u, :].bitcast(F32)
+
+            return words_of
 
         def weight_tiles(label, columns):
             grouped = fixed.tile([P, columns, PACK], BF16, name=label + "_grouped", align_bytes=64)

@@ -17,6 +17,7 @@ SUBS = 4
 TILE = SUBS * P
 LORA_SCALE = 2.0
 QUARTER = 64
+VECTOR_SORTS_FROM = 6
 SORTED = 2
 OUT_LAG = 2
 
@@ -36,7 +37,7 @@ def tile_replaced_compose_lora_pa_t_kernel(tc, x, lora_A, lora_B, W, bias, lora_
     with ExitStack() as ctx:
         fixed = ctx.enter_context(tc.tile_pool(name="fixed", bufs=1))
         x_pool = ctx.enter_context(tc.tile_pool(name="x_pool", bufs=n_tiles))
-        sorted_pool = ctx.enter_context(tc.tile_pool(name="sorted_pool", bufs=2))
+        sorted_pool = ctx.enter_context(tc.tile_pool(name="sorted_pool", bufs=3))
         grouped_pool = ctx.enter_context(tc.tile_pool(name="grouped_pool", bufs=2))
         codes_pool = ctx.enter_context(tc.tile_pool(name="codes_pool", bufs=OUT_LAG + 3))
         result_pool = ctx.enter_context(tc.tile_pool(name="result_pool", bufs=2 * n_tiles + 1))
@@ -122,14 +123,6 @@ def tile_replaced_compose_lora_pa_t_kernel(tc, x, lora_A, lora_B, W, bias, lora_
             return lambda s, u: rows[:, s, :].bitcast(F32)[:, u : HALVES * P : HALVES]
 
         def sort_x(i):
-            x_sorted = sorted_pool.tile([P, SORTED, HALVES, P], F32, name="x_sorted")
-            nc.vector.tensor_copy(
-                out=x_sorted[:].rearrange("c s u p -> c s p u"),
-                in_=x_in[i][:, SUBS - SORTED :, :]
-                .rearrange("c s d -> c (s d)")
-                .bitcast(F32)
-                .rearrange("c (s p u) -> c s p u", s=SORTED, u=HALVES),
-            )
             x_pairs = sorted_pool.tile([P, SUBS - SORTED, HALVES, 2 * P], BF16, name="x_pairs")
             for s in range(SUBS - SORTED):
                 nc.gpsimd.tensor_scalar(
@@ -140,13 +133,18 @@ def tile_replaced_compose_lora_pa_t_kernel(tc, x, lora_A, lora_B, W, bias, lora_
                     op0=mybir.AluOpType.mult,
                     op1=mybir.AluOpType.add,
                 )
-
-            def words_of(s, u):
-                if s >= SUBS - SORTED:
-                    return x_sorted[:, s - (SUBS - SORTED), u, :]
-                return x_pairs[:, s, u, :].bitcast(F32)
-
-            return words_of
+            others = as_loaded(x_in[i])
+            if i >= VECTOR_SORTS_FROM:
+                x_sorted = sorted_pool.tile([P, SORTED, HALVES, P], F32, name="x_sorted")
+                nc.vector.tensor_copy(
+                    out=x_sorted[:].rearrange("c s u p -> c s p u"),
+                    in_=x_in[i][:, SUBS - SORTED :, :]
+                    .rearrange("c s d -> c (s d)")
+                    .bitcast(F32)
+                    .rearrange("c (s p u) -> c s p u", s=SORTED, u=HALVES),
+                )
+                others = lambda s, u: x_sorted[:, s - (SUBS - SORTED), u, :]
+            return lambda s, u: x_pairs[:, s, u, :].bitcast(F32) if s < SUBS - SORTED else others(s, u)
 
         def weight_tiles(label, columns):
             grouped = fixed.tile([P, columns, PACK], BF16, name=label + "_grouped", align_bytes=64)
@@ -262,8 +260,6 @@ def tile_replaced_compose_lora_pa_t_kernel(tc, x, lora_A, lora_B, W, bias, lora_
         def step(j, before_quantising=None):
             has_h = 0 <= j < n_tiles
             has_x = 0 <= j + 2 < n_tiles
-            if 0 < j < n_tiles - 3:
-                x_words[j + 3] = sort_x(j + 3)
             if has_h or has_x:
                 grouped, codes, scales = step_tiles()
             if has_h:
@@ -271,13 +267,14 @@ def tile_replaced_compose_lora_pa_t_kernel(tc, x, lora_A, lora_B, W, bias, lora_
                 h_mx[j] = (codes[:, 0], scales[:, 0])
             if has_x:
                 place = (psum_o, "out_bank") if j < 0 else (psum_t, "x_bank")
-                warm = 1 if j < 0 else 0
                 by_turns = nc.scalar.copy if j > 0 and j % 3 == 2 else nc.vector.tensor_copy
-                turn_bank(x_words[j + 2], 0, grouped[:, 1], *place, nc.scalar.copy, warm)
-                turn_bank(x_words[j + 2], 1, grouped[:, 1], *place, by_turns, warm)
+                turn_bank(x_words[j + 2], 0, grouped[:, 1], *place, nc.scalar.copy)
+                turn_bank(x_words[j + 2], 1, grouped[:, 1], *place, by_turns)
                 x_mx[j + 2] = (codes[:, 1], scales[:, 1])
             if 0 <= j - OUT_LAG:
                 out_passes(j - OUT_LAG)
+            if 0 <= j < n_tiles - 4:
+                x_words[j + 4] = sort_x(j + 4)
             if before_quantising:
                 before_quantising()
             if has_h or has_x:

from contextlib import ExitStack

import concourse.mybir as mybir
from concourse.masks import make_identity

F32 = mybir.dt.float32
BF16 = mybir.dt.bfloat16
U32 = mybir.dt.uint32
U8 = mybir.dt.uint8
FP8X4 = mybir.dt.float8_e4m3fn_x4

P = 128
PACK = 4
K = P * PACK
HALVES = 2
SUBS = 4
TILE = SUBS * P
LORA_SCALE = 2.0
QUARTER = 64
VECTOR_SORTS_FROM = 6
SORTED = 2
OUT_LAG = 2

FLOPS = 2 * 8192 * 512 * (512 + 256 + 256)


def tile_replaced_compose_lora_pa_t_kernel(tc, x, lora_A, lora_B, W, bias, lora_weights, out):
    nc = tc.nc
    x_rows = x.flatten_outer_dims()
    out_rows = out.flatten_outer_dims()
    a_rows = lora_A.flatten_outer_dims()
    rank = lora_A.shape[1]
    d_out = W.shape[0]
    n_tiles = x_rows.shape[0] // TILE
    assert x_rows.shape[1] == K and a_rows.shape[0] == K and d_out == 2 * P

    with ExitStack() as ctx:
        fixed = ctx.enter_context(tc.tile_pool(name="fixed", bufs=1))
        x_pool = ctx.enter_context(tc.tile_pool(name="x_pool", bufs=n_tiles))
        sorted_pool = ctx.enter_context(tc.tile_pool(name="sorted_pool", bufs=3))
        grouped_pool = ctx.enter_context(tc.tile_pool(name="grouped_pool", bufs=2))
        codes_pool = ctx.enter_context(tc.tile_pool(name="codes_pool", bufs=OUT_LAG + 3))
        result_pool = ctx.enter_context(tc.tile_pool(name="result_pool", bufs=2 * n_tiles + 1))
        psum_t = ctx.enter_context(tc.psum_pool(name="psum_t", bufs=2))
        psum_h = ctx.enter_context(tc.psum_pool(name="psum_h", bufs=4))
        psum_o = ctx.enter_context(tc.psum_pool(name="psum_o", bufs=2))
        ctx.enter_context(tc.manual_schedule())

        ident = fixed.tile([P, P], F32)
        make_identity(nc, ident[:])

        def load_x(i):
            x_tile = x_pool.tile([P, SUBS, K], BF16, name="x_tile")
            nc.sync.dma_start(
                out=x_tile[:],
                in_=x_rows[i * TILE : (i + 1) * TILE, :].rearrange("(c s) d -> c s d", s=SUBS),
            )
            return x_tile

        x_first = x_pool.tile([P, SUBS, K], BF16, name="x_tile")
        a_in = fixed.tile([P, PACK, K], BF16)
        for half in (slice(0, 2), slice(2, 4)):
            nc.sync.dma_start(
                out=x_first[:, half, :], in_=x_rows[:TILE, :].rearrange("(c s) d -> c s d", s=SUBS)[:, half, :]
            )
            nc.sync.dma_start(out=a_in[:, half, :], in_=a_rows.rearrange("(c t) d -> c t d", t=PACK)[:, half, :])
        x_in = [x_first, load_x(1)]
        b_in = fixed.tile([P, QUARTER * rank], BF16)
        nc.sync.dma_start(out=b_in[:], in_=lora_B.rearrange("n (oh ol) r -> (n oh) (ol r)", ol=QUARTER))
        w_in = fixed.tile([P, 2, K], BF16)
        nc.sync.dma_start(out=w_in[:], in_=W.rearrange("(s c) d -> c s d", c=P))
        n_adapters = lora_weights.shape[0]
        rows = fixed.tile([P, d_out + n_adapters], BF16, name="rows")
        nc.gpsimd.memset(rows[:], 0.0)
        nc.sync.dma_start(out=rows[0:1, :d_out], in_=bias.rearrange("(one o) -> one o", one=1))
        nc.sync.dma_start(out=rows[0:1, d_out:], in_=lora_weights.rearrange("(one n) -> one n", one=1))
        ones = fixed.tile([P, P], BF16, name="ones")
        nc.gpsimd.memset(ones[:], 1.0)
        x_in.extend([load_x(i) for i in range(2, n_tiles)])

        bias_all = fixed.tile([P, d_out], F32, name="bias_all")
        bias_twice = bias_all[:].unsqueeze(1).to_broadcast([P, 2, d_out])
        mix = fixed.tile([P, 1], F32, name="mix")
        mix_row = fixed.tile([P, n_adapters, PACK], BF16, name="mix_row")

        def spread_vectors():
            bank = psum_o.tile([P, d_out + 1], F32, name="vector_bank", tag="out_bank")
            nc.tensor.matmul(out=bank[:, :d_out], lhsT=ones[:], rhs=rows[:, :d_out], start=True, stop=True)
            nc.tensor.matmul(
                out=bank[:, d_out:],
                lhsT=mix_row[:].rearrange("p n a -> p (n a)"),
                rhs=ones[:, 0:1],
                start=True,
                stop=True,
            )
            nc.vector.tensor_copy(out=mix[:], in_=bank[:, d_out:])
            nc.scalar.copy(out=bias_all[:], in_=bank[:, :d_out])

        def quantise(grouped, codes, scales):
            nc.vector.quantize_mx(out=codes.bitcast(FP8X4), scales=scales, in_=grouped)

        zeros = fixed.tile([P, K // 2], F32, name="zeros")
        nc.vector.memset(zeros[:], 0.0)
        warm_in = zeros[:].bitcast(BF16)
        warm_bank = psum_h.tile([P, K], F32, name="warm_bank", tag="h_bank")

        def keep_warm(count):
            for turn in range(count):
                nc.tensor.matmul(out=warm_bank[:], lhsT=warm_in[:, :P], rhs=warm_in, start=True, stop=True)

        def turn_bank(words_of, pair, grouped, psum, bank_tag, leave, warm=0):
            bank = psum.tile([P, HALVES, 2, P], F32, name="turn_bank", tag=bank_tag)
            for s in range(2):
                for u in range(HALVES):
                    nc.tensor.transpose(out=bank[:, u, s, :], in_=words_of(2 * pair + s, u), identity=ident[:])
            keep_warm(warm)
            leave(
                out=grouped.bitcast(F32)[:, 2 * pair * P : 2 * (pair + 1) * P, :],
                in_=bank[:].rearrange("p u s c -> p (s c) u"),
            )

        def as_loaded(rows):
            return lambda s, u: rows[:, s, :].bitcast(F32)[:, u : HALVES * P : HALVES]

        def sort_x(i):
            x_pairs = sorted_pool.tile([P, SUBS - SORTED, HALVES, 2 * P], BF16, name="x_pairs")
            for s in range(SUBS - SORTED):
                nc.gpsimd.tensor_scalar(
                    out=x_pairs[:, s].rearrange("c u (p e) -> c u p e", e=2),
                    in0=x_in[i][:, s, :].rearrange("c (p u e) -> c u p e", u=HALVES, e=2),
                    scalar1=1.0,
                    scalar2=0.0,
                    op0=mybir.AluOpType.mult,
                    op1=mybir.AluOpType.add,
                )
            others = as_loaded(x_in[i])
            if i >= VECTOR_SORTS_FROM:
                x_sorted = sorted_pool.tile([P, SORTED, HALVES, P], F32, name="x_sorted")
                nc.vector.tensor_copy(
                    out=x_sorted[:].rearrange("c s u p -> c s p u"),
                    in_=x_in[i][:, SUBS - SORTED :, :]
                    .rearrange("c s d -> c (s d)")
                    .bitcast(F32)
                    .rearrange("c (s p u) -> c s p u", s=SORTED, u=HALVES),
                )
                others = lambda s, u: x_sorted[:, s - (SUBS - SORTED), u, :]
            return lambda s, u: x_pairs[:, s, u, :].bitcast(F32) if s < SUBS - SORTED else others(s, u)

        def weight_tiles(label, columns):
            grouped = fixed.tile([P, columns, PACK], BF16, name=label + "_grouped", align_bytes=64)
            codes = fixed.tile([P, columns], U32, name=label + "_codes", align_bytes=64)
            scales = fixed.tile([P, columns], U8, name=label + "_scales", align_bytes=64)
            return grouped[:], codes[:], scales[:]

        def quantise_columns(tiles, columns):
            grouped, codes, scales = tiles
            quantise(grouped[:, columns, :].rearrange("p c t -> p (c t)"), codes[:, columns], scales[:, columns])

        def sort_b():
            b_sorted = fixed.tile([P, PACK, P], F32)
            nc.scalar.copy(
                out=b_sorted[:].rearrange("q a (ol w) -> q a ol w", w=2),
                in_=b_in[:].bitcast(F32).rearrange("q (ol a w) -> q a ol w", a=PACK, w=2),
            )
            return b_sorted

        def turn_b_first(b_sorted):
            bank = psum_o.tile([P, PACK, P], F32, name="b_bank_first", tag="out_bank")
            for a in range(PACK):
                nc.tensor.transpose(out=bank[:, a, :], in_=b_sorted[:, a, :], identity=ident[:])
            b_turned = fixed.tile([P, PACK, P], F32)
            nc.vector.tensor_copy(
                out=b_turned[:].rearrange("v oh (n a) -> v oh n a", a=PACK),
                in_=bank[:].rearrange("v a (n oh) -> v oh n a", oh=PACK),
            )
            return b_turned

        def turn_b_second(b_turned):
            bank = psum_o.tile([P, PACK, P], F32, name="b_bank_second", tag="out_bank")
            for oh in range(PACK):
                nc.tensor.transpose(out=bank[:, oh, :], in_=b_turned[:, oh, :], identity=ident[:])
            b_grouped = fixed.tile([P, d_out * PACK], BF16, align_bytes=64)
            nc.vector.tensor_scalar(
                out=b_grouped[:],
                in0=bank[:].bitcast(BF16).rearrange("q oh v -> q (oh v)"),
                scalar1=mix[:, 0:1],
                scalar2=LORA_SCALE,
                op0=mybir.AluOpType.mult,
                op1=mybir.AluOpType.mult,
            )
            codes = fixed.tile([P, d_out], U32, name="b_codes", align_bytes=64)
            scales = fixed.tile([P, d_out], U8, name="b_scales", align_bytes=64)
            quantise(b_grouped[:], codes[:], scales[:])
            return codes, scales

        x_words = {i: as_loaded(x_in[i]) for i in range(n_tiles)}
        x_mx = {}
        h_mx = {}

        def low_rank_passes(i, h_grouped):
            x_codes, x_scales = x_mx[i]
            for s in range(SUBS):
                tokens = slice(s * P, (s + 1) * P)
                bank = psum_h.tile([P, PACK, P], F32, name="h_bank", tag="h_bank")
                for t in range(PACK):
                    ks = slice(t * P, (t + 1) * P)
                    nc.tensor.matmul_mx(
                        out=bank[:, t, :],
                        lhsT=a_codes[:, ks].bitcast(FP8X4),
                        lhsT_scale=a_scales[:, ks],
                        rhs=x_codes[:, tokens].bitcast(FP8X4),
                        rhs_scale=x_scales[:, tokens],
                        start=True,
                        stop=True,
                    )
                nc.scalar.copy(out=h_grouped[:, tokens, :], in_=bank[:].rearrange("p t c -> p c t"))

        def out_passes(i):
            x_codes, x_scales = x_mx[i]
            h_codes, h_scales = h_mx[i]
            out_tile = out_rows[i * TILE : (i + 1) * TILE, :].rearrange("(c s) o -> c s o", s=SUBS)
            splits = ((0, 2), (2, 3), (3, 4)) if i == n_tiles - 1 else ((0, 2), (2, 4))
            for number, (first, end) in enumerate(splits):
                free = number == 1 and i >= n_tiles - OUT_LAG - 2
                bank = (psum_t if free else psum_o).tile(
                    [P, end - first, d_out], F32, name="out_bank", tag="x_bank" if free else "out_bank"
                )
                for s in range(first, end):
                    tokens = slice(s * P, (s + 1) * P)
                    nc.tensor.matmul_mx(
                        out=bank[:, s - first, :],
                        lhsT=x_codes[:, tokens].bitcast(FP8X4),
                        lhsT_scale=x_scales[:, tokens],
                        rhs=w_codes[:].bitcast(FP8X4),
                        rhs_scale=w_scales[:],
                        start=True,
                        stop=False,
                    )
                    nc.tensor.matmul_mx(
                        out=bank[:, s - first, :],
                        lhsT=h_codes[:, tokens].bitcast(FP8X4),
                        lhsT_scale=h_scales[:, tokens],
                        rhs=b_codes[:].bitcast(FP8X4),
                        rhs_scale=b_scales[:],
                        start=False,
                        stop=True,
                    )
                result = result_pool.tile([P, end - first, d_out], F32, name="result")
                nc.vector.tensor_tensor(
                    out=result[:], in0=bank[:], in1=bias_twice[:, : end - first, :], op=mybir.AluOpType.add
                )
                nc.sync.dma_start(out=out_tile[:, first:end, :], in_=result[:])

        def step_tiles():
            grouped = grouped_pool.tile([P, 2, TILE, PACK], BF16, name="grouped", align_bytes=64)
            codes = codes_pool.tile([P, 2, TILE], U32, name="codes", align_bytes=64)
            scales = codes_pool.tile([P, 2, TILE], U8, name="scales", align_bytes=64)
            return grouped, codes, scales

        def step(j, before_quantising=None):
            has_h = 0 <= j < n_tiles
            has_x = 0 <= j + 2 < n_tiles
            if has_h or has_x:
                grouped, codes, scales = step_tiles()
            if has_h:
                low_rank_passes(j, grouped[:, 0])
                h_mx[j] = (codes[:, 0], scales[:, 0])
            if has_x:
                place = (psum_o, "out_bank") if j < 0 else (psum_t, "x_bank")
                by_turns = nc.scalar.copy if j > 0 and j % 3 == 2 else nc.vector.tensor_copy
                turn_bank(x_words[j + 2], 0, grouped[:, 1], *place, nc.scalar.copy)
                turn_bank(x_words[j + 2], 1, grouped[:, 1], *place, by_turns)
                x_mx[j + 2] = (codes[:, 1], scales[:, 1])
            if 0 <= j - OUT_LAG:
                out_passes(j - OUT_LAG)
            if 0 <= j < n_tiles - 4:
                x_words[j + 4] = sort_x(j + 4)
            if before_quantising:
                before_quantising()
            if has_h or has_x:
                filled = slice(0 if has_h else 1, 2 if has_x else 1)
                quantise(
                    grouped[:, filled].rearrange("p g c t -> p (g c t)"),
                    codes[:, filled].rearrange("p g c -> p (g c)"),
                    scales[:, filled].rearrange("p g c -> p (g c)"),
                )

        grouped, codes, scales = step_tiles()
        x_mx[0] = (codes[:, 1], scales[:, 1])
        x_tiles = (grouped[:, 1], codes[:, 1], scales[:, 1])
        a_tiles = weight_tiles("a", K)
        a_codes, a_scales = a_tiles[1:]
        halves = (slice(0, 2 * P), slice(2 * P, 4 * P))
        keep_warm(4)
        turn_bank(x_words[0], 0, x_tiles[0], psum_t, "x_bank", nc.vector.tensor_copy, warm=1)
        turn_bank(as_loaded(a_in), 0, a_tiles[0], psum_h, "h_bank", nc.scalar.copy, warm=1)
        quantise_columns(x_tiles, halves[0])
        turn_bank(x_words[0], 1, x_tiles[0], psum_t, "x_bank", nc.vector.tensor_copy, warm=1)
        turn_bank(as_loaded(a_in), 1, a_tiles[0], psum_h, "h_bank", nc.scalar.copy, warm=1)
        quantise_columns(a_tiles, halves[0])
        quantise_columns(x_tiles, halves[1])
        quantise_columns(a_tiles, halves[1])
        step(-1)
        b_sorted = sort_b()
        weights = {}
        w_tiles = weight_tiles("w", d_out)
        w_codes, w_scales = w_tiles[1:]

        def first_turns():
            weights["b_turned"] = turn_b_first(b_sorted)
            turn_bank(as_loaded(w_in), 0, w_tiles[0], psum_o, "out_bank", nc.vector.tensor_copy)
            nc.vector.tensor_copy(out=mix_row[:], in_=rows[:, d_out:].unsqueeze(2).to_broadcast([P, n_adapters, PACK]))

        def second_turn():
            spread_vectors()
            weights["b"] = turn_b_second(weights["b_turned"])

        step(0, first_turns)
        quantise_columns(w_tiles, slice(0, d_out))
        step(1, second_turn)
        b_codes, b_scales = weights["b"]
        for j in range(2, n_tiles + OUT_LAG):
            step(j)
